import numpy as np
import ml_dtypes


def mxq(x, axis, fmt="e4m3"):
    dtype, down = {"e4m3": (ml_dtypes.float8_e4m3fn, 7), "e5m2": (ml_dtypes.float8_e5m2, 14)}[fmt]
    v = np.moveaxis(np.asarray(x, np.float32).astype(ml_dtypes.bfloat16).astype(np.float64), axis, -1)
    blocks = v.reshape(v.shape[:-1] + (-1, 32))
    amax = np.abs(blocks).max(-1, keepdims=True)
    byte = np.maximum(np.where(amax > 0, np.frexp(amax)[1] - 1 + 127, 0) - down, 1)
    scale = np.exp2(byte - 127.0)
    codes = (blocks / scale).astype(np.float32).astype(dtype).astype(np.float64)
    return np.moveaxis((codes * scale).reshape(v.shape), -1, axis)


WIDE = False


def mx_kscale(k):
    if not WIDE:
        return np.ones(k)
    levels = np.array([10, -10, 5, -5, 0])
    a = np.random.permutation(np.resize(levels, k // 512 * 4)).reshape(k // 512, 4)
    idx = np.arange(k)
    return np.exp2(a[idx // 512, idx % 128 // 32])


BF16 = ml_dtypes.bfloat16


def bf(x):
    return np.asarray(x, np.float32).astype(BF16)


def f64(x):
    return np.asarray(x).astype(np.float64)


B, N, HID, ITERS = 256, 64, 1024, 10
DIN = 2 * N * N
SLOPE = 0.01


def leaky(v):
    return np.where(v >= 0.0, v, SLOPE * v)


def setup_inputs():
    s, t = mx_kscale(DIN), mx_kscale(HID)
    sp, sq = s[0::2].reshape(N, N), s[1::2].reshape(N, N)
    return {"p": bf(np.random.uniform(size=(B, N, N)) * sp),
            "q": bf(np.random.uniform(size=(B, N, N)) * sq),
            "W1": bf(np.random.standard_normal((DIN, HID)) * 1.7 / np.sqrt(DIN) / s[:, None] * t),
            "b1": bf(np.random.standard_normal(HID) * 0.3 * t),
            "W2": bf(np.random.standard_normal((HID, HID)) * 1.4 / np.sqrt(HID) / t[:, None]),
            "b2": bf(np.random.standard_normal(HID) * 0.3)}


def reference(p, q, W1, b1, W2, b2):
    x = np.stack([f64(p), f64(q)], axis=-1).reshape(B, DIN)
    h1 = leaky((mxq(x, 1, "e4m3") @ mxq(f64(W1), 0, "e4m3")) + f64(b1))
    return leaky((mxq(h1, 1, "e4m3") @ mxq(f64(W2), 0, "e4m3")) + f64(b2))

@@ -1,0 +1,226 @@
+from contextlib import ExitStack
+
+import concourse.mybir as mybir
+from concourse.masks import make_identity
+
+F32 = mybir.dt.float32
+BF16 = mybir.dt.bfloat16
+U32 = mybir.dt.uint32
+U8 = mybir.dt.uint8
+FP8X4 = mybir.dt.float8_e4m3fn_x4
+ALU = mybir.AluOpType
+ACT = mybir.ActivationFunctionType
+
+P = 128
+PACK = 4
+K_PASS = P * PACK
+BATCH = 256
+TABLE = 64 * 64
+DIN = 2 * TABLE
+HID = 1024
+SLOPE = 0.01
+SAMPLE_TILES = BATCH // P
+PASSES1 = DIN // K_PASS
+PASSES2 = HID // K_PASS
+HID_TILES = HID // P
+BANK = 512
+RUN = 4
+VECTOR_COLS = 480
+LAST_PIECES = 4
+
+FLOPS = 2 * BATCH * DIN * HID + 2 * BATCH * HID * HID
+
+
+def tile_matchingnet_pb_k_kernel(tc, p, q, W1, b1, W2, b2, out):
+    nc = tc.nc
+    with ExitStack() as ctx:
+        const = ctx.enter_context(tc.tile_pool(name="const", bufs=1))
+        x_pool = ctx.enter_context(tc.tile_pool(name="x", bufs=1))
+        raw_pool = ctx.enter_context(tc.tile_pool(name="raw", bufs=6))
+        grouped_pool = ctx.enter_context(tc.tile_pool(name="grouped", bufs=3))
+        w1_pool = ctx.enter_context(tc.tile_pool(name="w1", bufs=3))
+        w2_pool = ctx.enter_context(tc.tile_pool(name="w2", bufs=1))
+        h_pool = ctx.enter_context(tc.tile_pool(name="h", bufs=1))
+        out_pool = ctx.enter_context(tc.tile_pool(name="outs", bufs=4))
+        psum = ctx.enter_context(tc.psum_pool(name="psum", bufs=8))
+        ctx.enter_context(tc.manual_schedule())
+
+        b1_rows = const.tile([P, P], BF16)
+        nc.vector.memset(b1_rows[:], 0.0)
+        nc.sync.dma_start(out=b1_rows[0:HID_TILES, :], in_=b1.rearrange("(i c) -> i c", c=P))
+        b2_row = const.tile([P, HID], BF16)
+        nc.vector.memset(b2_row[:], 0.0)
+        nc.sync.dma_start(out=b2_row[0:1, :], in_=b2.rearrange("(o n) -> o n", o=1))
+
+        p_tiles = p.rearrange("(m b) i j -> m b (i j)", b=P)
+        q_tiles = q.rearrange("(m b) i j -> m b (i j)", b=P)
+        tables = []
+        for m in range(SAMPLE_TILES):
+            both = x_pool.tile([P, 2, TABLE], BF16, name="tables%d" % m)
+            for half in range(2):
+                cols = slice(half * TABLE // 2, (half + 1) * TABLE // 2)
+                nc.sync.dma_start(out=both[:, 0, cols], in_=p_tiles[m][:, cols])
+                nc.sync.dma_start(out=both[:, 1, cols], in_=q_tiles[m][:, cols])
+            tables.append(both)
+
+        ident = const.tile([P, P], F32)
+        make_identity(nc, ident[:])
+        ones = const.tile([P, P], BF16)
+        nc.vector.memset(ones[:], 1.0)
+
+        b1_f32 = const.tile([P, P], F32)
+        nc.vector.tensor_copy(out=b1_f32[:], in_=b1_rows[:])
+        b1_ps = psum.tile([P, P], F32, tag="bank")
+        nc.tensor.transpose(b1_ps[:], b1_f32[:], ident[:])
+        b1_col = const.tile([P, HID_TILES], F32)
+        nc.vector.tensor_copy(out=b1_col[:], in_=b1_ps[:, 0:HID_TILES])
+
+        b2_all = const.tile([P, HID], F32)
+        for half in range(HID // BANK):
+            cols = slice(half * BANK, (half + 1) * BANK)
+            b2_ps = psum.tile([P, BANK], F32, tag="bank")
+            nc.tensor.matmul(out=b2_ps[:], lhsT=ones[:], rhs=b2_row[:, cols], start=True, stop=True)
+            nc.scalar.activation(out=b2_all[:, cols], in_=b2_ps[:], func=ACT.Identity, scale=1.0)
+
+        x_grouped = x_pool.tile([P, PASSES1, BATCH, PACK], BF16, align_bytes=64)
+        x_codes = x_pool.tile([P, PASSES1, BATCH], U32, align_bytes=64)
+        x_scales = x_pool.tile([P, PASSES1, BATCH], U8, align_bytes=64)
+        x_grouped_words = x_grouped[:].bitcast(F32)
+
+        def quantise_x(pair, samples):
+            for g in (2 * pair, 2 * pair + 1):
+                nc.vector.quantize_mx(
+                    out=x_codes[:, g, samples].bitcast(FP8X4),
+                    scales=x_scales[:, g, samples],
+                    in_=x_grouped[:, g, samples, :].rearrange("a n t -> a (n t)"),
+                )
+
+        for m in range(SAMPLE_TILES):
+            samples = slice(m * P, (m + 1) * P)
+            words = tables[m][:].bitcast(F32)
+            for pair in range(PASSES1 // 2):
+                xt = psum.tile([P, 2, 2, P], F32, tag="bank")
+                for gg in range(2):
+                    g = 2 * pair + gg
+                    for s in range(2):
+                        nc.tensor.transpose(xt[:, gg, s, :], words[:, s, g * P : (g + 1) * P], ident[:])
+                nc.scalar.copy(
+                    out=x_grouped_words[:, 2 * pair : 2 * pair + 2, samples, :],
+                    in_=xt[:].rearrange("a g s n -> a g n s"),
+                )
+                if pair > 0:
+                    quantise_x(pair - 1, samples)
+            quantise_x(PASSES1 // 2 - 1, samples)
+
+        w1_chunks = W1.rearrange("(c a j) n -> c a j n", a=P, j=PACK)
+        w2_chunks = W2.rearrange("(g t a) n -> g a t n", t=PACK, a=P)
+        w2_codes = w2_pool.tile([P, PASSES2, HID], U32, align_bytes=64)
+        w2_scales = w2_pool.tile([P, PASSES2, HID], U8, align_bytes=64)
+        acc = [psum.tile([P, BATCH], F32, tag="bank", name="acc%d" % i) for i in range(HID_TILES)]
+        h_grouped = h_pool.tile([P, PASSES2, BATCH, PACK], BF16, align_bytes=64)
+        h_codes = h_pool.tile([P, PASSES2, BATCH], U32, align_bytes=64)
+        h_scales = h_pool.tile([P, PASSES2, BATCH], U8, align_bytes=64)
+        biased = [h_pool.tile([P, PACK, BATCH], F32, name="biased%d" % g) for g in range(PASSES2)]
+
+        last_width = HID // LAST_PIECES
+        pieces = [("W2", g, 0, HID) for g in range(PASSES2)]
+        pieces += [("W1", c, 0, HID) for c in range(PASSES1 - 1)]
+        pieces += [("W1", PASSES1 - 1, j * last_width, last_width) for j in range(LAST_PIECES)]
+
+        def load_and_regroup(matrix, chunk, first, width):
+            raw = raw_pool.tile([P, PACK, width], BF16, tag="raw", name="raw")
+            grouped = grouped_pool.tile([P, width, PACK], BF16, align_bytes=64, tag="grouped", name="grouped")
+            if matrix == "W1":
+                nc.sync.dma_start(out=raw[:], in_=w1_chunks[chunk][:, :, first : first + width])
+                rows = raw[:].rearrange("a (e s) n -> a s e n", s=2)
+            else:
+                nc.sync.dma_start(out=raw[:], in_=w2_chunks[chunk][:, :, first : first + width])
+                rows = raw[:].rearrange("a (s e) n -> a s e n", s=2)
+            split = width * VECTOR_COLS // HID
+            nc.vector.tensor_copy(
+                out=grouped[:, 0:split, :].rearrange("a (c i) (s e) -> a c s e i", i=RUN, s=2),
+                in_=rows[:, :, :, 0:split].rearrange("a s e (c i) -> a c s e i", i=RUN),
+            )
+            nc.scalar.copy(
+                out=grouped[:, split:width, :].rearrange("a (c i) (s e) -> a c s e i", i=RUN, s=2),
+                in_=rows[:, :, :, split:width].rearrange("a s e (c i) -> a c s e i", i=RUN),
+            )
+            return grouped
+
+        def quantise_and_multiply(matrix, chunk, first, width, grouped):
+            if matrix == "W2":
+                codes = w2_codes[:, chunk, :]
+                scales = w2_scales[:, chunk, :]
+            else:
+                codes = w1_pool.tile([P, width], U32, align_bytes=64, tag="codes", name="w1_codes")[:]
+                scales = w1_pool.tile([P, width], U8, align_bytes=64, tag="scales", name="w1_scales")[:]
+            nc.vector.quantize_mx(
+                out=codes.bitcast(FP8X4), scales=scales, in_=grouped[:].rearrange("a n t -> a (n t)")
+            )
+            if matrix == "W2":
+                return
+            for u in range(width // P):
+                i = first // P + u
+                units = slice(u * P, (u + 1) * P)
+                nc.tensor.matmul_mx(
+                    out=acc[i][:],
+                    lhsT=codes[:, units].bitcast(FP8X4),
+                    lhsT_scale=scales[:, units],
+                    rhs=x_codes[:, chunk, :].bitcast(FP8X4),
+                    rhs_scale=x_scales[:, chunk, :],
+                    start=(chunk == 0),
+                    stop=(chunk == PASSES1 - 1),
+                )
+                if chunk == PASSES1 - 1:
+                    nc.scalar.activation(
+                        out=biased[i // PACK][:, i % PACK, :],
+                        in_=acc[i][:],
+                        func=ACT.Identity,
+                        bias=b1_col[:, i : i + 1],
+                        scale=1.0,
+                    )
+
+        waiting = None
+        for k in range(len(pieces)):
+            grouped = load_and_regroup(*pieces[k])
+            if k > 0:
+                quantise_and_multiply(*pieces[k - 1], waiting)
+            waiting = grouped
+        quantise_and_multiply(*pieces[-1], waiting)
+
+        out_ps = [psum.tile([P, BANK], F32, tag="bank", name="out_ps%d" % b) for b in range(4)]
+        for g in range(PASSES2):
+            by_sample = biased[g][:].rearrange("a t n -> a n t")
+            nc.vector.scalar_tensor_tensor(
+                out=h_grouped[:, g, :, :], in0=by_sample, scalar=SLOPE, in1=by_sample, op0=ALU.mult, op1=ALU.max
+            )
+            nc.vector.quantize_mx(
+                out=h_codes[:, g, :].bitcast(FP8X4),
+                scales=h_scales[:, g, :],
+                in_=h_grouped[:, g, :, :].rearrange("a n t -> a (n t)"),
+            )
+            for m in range(SAMPLE_TILES):
+                samples = slice(m * P, (m + 1) * P)
+                for half in range(HID // BANK):
+                    cols = slice(half * BANK, (half + 1) * BANK)
+                    nc.tensor.matmul_mx(
+                        out=out_ps[2 * m + half][:],
+                        lhsT=h_codes[:, g, samples].bitcast(FP8X4),
+                        lhsT_scale=h_scales[:, g, samples],
+                        rhs=w2_codes[:, g, cols].bitcast(FP8X4),
+                        rhs_scale=w2_scales[:, g, cols],
+                        start=(g == 0),
+                        stop=(g == PASSES2 - 1),
+                    )
+
+        for m in range(SAMPLE_TILES):
+            samples = slice(m * P, (m + 1) * P)
+            for half in range(HID // BANK):
+                cols = slice(half * BANK, (half + 1) * BANK)
+                summed = out_pool.tile([P, BANK], F32)
+                nc.vector.tensor_tensor(out=summed[:], in0=out_ps[2 * m + half][:], in1=b2_all[:, cols], op=ALU.add)
+                result = out_pool.tile([P, BANK], F32)
+                nc.vector.scalar_tensor_tensor(
+                    out=result[:], in0=summed[:], scalar=SLOPE, in1=summed[:], op0=ALU.mult, op1=ALU.max
+                )
+                nc.sync.dma_start(out=out[samples, cols], in_=result[:])

@@ -25,7 +25,7 @@ PASSES2 = HID // K_PASS
 HID_TILES = HID // P
 BANK = 512
 RUN = 4
-VECTOR_COLS = 480
+VECTOR_COLS = 512
 LAST_PIECES = 4
 
 FLOPS = 2 * BATCH * DIN * HID + 2 * BATCH * HID * HID
@@ -104,7 +104,8 @@ def tile_matchingnet_pb_k_kernel(tc, p, q, W1, b1, W2, b2, out):
                     g = 2 * pair + gg
                     for s in range(2):
                         nc.tensor.transpose(xt[:, gg, s, :], words[:, s, g * P : (g + 1) * P], ident[:])
-                nc.scalar.copy(
+                copy = nc.vector.tensor_copy if pair % 4 == 3 else nc.scalar.copy
+                copy(
                     out=x_grouped_words[:, 2 * pair : 2 * pair + 2, samples, :],
                     in_=xt[:].rearrange("a g s n -> a g n s"),
                 )

@@ -14,6 +14,9 @@ ACT = mybir.ActivationFunctionType
 P = 128
 PACK = 4
 K_PASS = P * PACK
+BANK = 512
+PSUM_BANKS = 8
+
 BATCH = 256
 TABLE = 64 * 64
 DIN = 2 * TABLE
@@ -23,10 +26,14 @@ SAMPLE_TILES = BATCH // P
 PASSES1 = DIN // K_PASS
 PASSES2 = HID // K_PASS
 HID_TILES = HID // P
-BANK = 512
+OUT_BANKS = BATCH * HID // (P * BANK)
+
 RUN = 4
-VECTOR_COLS = 512
-LAST_PIECES = 4
+VECTOR_COLS = 496
+X_BANKS_PER_VECTOR_COPY = 4
+LAST_PIECES = 2
+RAW_BUFS = 6
+PIPE_BUFS = 3
 
 FLOPS = 2 * BATCH * DIN * HID + 2 * BATCH * HID * HID
 
@@ -36,18 +43,18 @@ def tile_matchingnet_pb_k_kernel(tc, p, q, W1, b1, W2, b2, out):
     with ExitStack() as ctx:
         const = ctx.enter_context(tc.tile_pool(name="const", bufs=1))
         x_pool = ctx.enter_context(tc.tile_pool(name="x", bufs=1))
-        raw_pool = ctx.enter_context(tc.tile_pool(name="raw", bufs=6))
-        grouped_pool = ctx.enter_context(tc.tile_pool(name="grouped", bufs=3))
-        w1_pool = ctx.enter_context(tc.tile_pool(name="w1", bufs=3))
+        raw_pool = ctx.enter_context(tc.tile_pool(name="raw", bufs=RAW_BUFS))
+        grouped_pool = ctx.enter_context(tc.tile_pool(name="grouped", bufs=PIPE_BUFS))
+        w1_pool = ctx.enter_context(tc.tile_pool(name="w1", bufs=PIPE_BUFS))
         w2_pool = ctx.enter_context(tc.tile_pool(name="w2", bufs=1))
         h_pool = ctx.enter_context(tc.tile_pool(name="h", bufs=1))
-        out_pool = ctx.enter_context(tc.tile_pool(name="outs", bufs=4))
-        psum = ctx.enter_context(tc.psum_pool(name="psum", bufs=8))
+        out_pool = ctx.enter_context(tc.tile_pool(name="outs", bufs=OUT_BANKS))
+        psum = ctx.enter_context(tc.psum_pool(name="psum", bufs=PSUM_BANKS))
         ctx.enter_context(tc.manual_schedule())
 
         b1_rows = const.tile([P, P], BF16)
         nc.vector.memset(b1_rows[:], 0.0)
-        nc.sync.dma_start(out=b1_rows[0:HID_TILES, :], in_=b1.rearrange("(i c) -> i c", c=P))
+        nc.sync.dma_start(out=b1_rows[0:HID_TILES, :], in_=b1.rearrange("(i a) -> i a", a=P))
         b2_row = const.tile([P, HID], BF16)
         nc.vector.memset(b2_row[:], 0.0)
         nc.sync.dma_start(out=b2_row[0:1, :], in_=b2.rearrange("(o n) -> o n", o=1))
@@ -83,9 +90,9 @@ def tile_matchingnet_pb_k_kernel(tc, p, q, W1, b1, W2, b2, out):
             nc.scalar.activation(out=b2_all[:, cols], in_=b2_ps[:], func=ACT.Identity, scale=1.0)
 
         x_grouped = x_pool.tile([P, PASSES1, BATCH, PACK], BF16, align_bytes=64)
+        x_grouped_words = x_grouped[:].bitcast(F32)
         x_codes = x_pool.tile([P, PASSES1, BATCH], U32, align_bytes=64)
         x_scales = x_pool.tile([P, PASSES1, BATCH], U8, align_bytes=64)
-        x_grouped_words = x_grouped[:].bitcast(F32)
 
         def quantise_x(pair, samples):
             for g in (2 * pair, 2 * pair + 1):
@@ -104,7 +111,10 @@ def tile_matchingnet_pb_k_kernel(tc, p, q, W1, b1, W2, b2, out):
                     g = 2 * pair + gg
                     for s in range(2):
                         nc.tensor.transpose(xt[:, gg, s, :], words[:, s, g * P : (g + 1) * P], ident[:])
-                copy = nc.vector.tensor_copy if pair % 4 == 3 else nc.scalar.copy
+                if pair % X_BANKS_PER_VECTOR_COPY == X_BANKS_PER_VECTOR_COPY - 1:
+                    copy = nc.vector.tensor_copy
+                else:
+                    copy = nc.scalar.copy
                 copy(
                     out=x_grouped_words[:, 2 * pair : 2 * pair + 2, samples, :],
                     in_=xt[:].rearrange("a g s n -> a g n s"),
@@ -118,9 +128,6 @@ def tile_matchingnet_pb_k_kernel(tc, p, q, W1, b1, W2, b2, out):
         w2_codes = w2_pool.tile([P, PASSES2, HID], U32, align_bytes=64)
         w2_scales = w2_pool.tile([P, PASSES2, HID], U8, align_bytes=64)
         acc = [psum.tile([P, BATCH], F32, tag="bank", name="acc%d" % i) for i in range(HID_TILES)]
-        h_grouped = h_pool.tile([P, PASSES2, BATCH, PACK], BF16, align_bytes=64)
-        h_codes = h_pool.tile([P, PASSES2, BATCH], U32, align_bytes=64)
-        h_scales = h_pool.tile([P, PASSES2, BATCH], U8, align_bytes=64)
         biased = [h_pool.tile([P, PACK, BATCH], F32, name="biased%d" % g) for g in range(PASSES2)]
 
         last_width = HID // LAST_PIECES
@@ -189,7 +196,10 @@ def tile_matchingnet_pb_k_kernel(tc, p, q, W1, b1, W2, b2, out):
             waiting = grouped
         quantise_and_multiply(*pieces[-1], waiting)
 
-        out_ps = [psum.tile([P, BANK], F32, tag="bank", name="out_ps%d" % b) for b in range(4)]
+        h_grouped = h_pool.tile([P, PASSES2, BATCH, PACK], BF16, align_bytes=64)
+        h_codes = h_pool.tile([P, PASSES2, BATCH], U32, align_bytes=64)
+        h_scales = h_pool.tile([P, PASSES2, BATCH], U8, align_bytes=64)
+        out_ps = [psum.tile([P, BANK], F32, tag="bank", name="out_ps%d" % b) for b in range(OUT_BANKS)]
         for g in range(PASSES2):
             by_sample = biased[g][:].rearrange("a t n -> a n t")
             nc.vector.scalar_tensor_tensor(
@@ -200,28 +210,34 @@ def tile_matchingnet_pb_k_kernel(tc, p, q, W1, b1, W2, b2, out):
                 scales=h_scales[:, g, :],
                 in_=h_grouped[:, g, :, :].rearrange("a n t -> a (n t)"),
             )
-            for m in range(SAMPLE_TILES):
-                samples = slice(m * P, (m + 1) * P)
-                for half in range(HID // BANK):
-                    cols = slice(half * BANK, (half + 1) * BANK)
-                    nc.tensor.matmul_mx(
-                        out=out_ps[2 * m + half][:],
-                        lhsT=h_codes[:, g, samples].bitcast(FP8X4),
-                        lhsT_scale=h_scales[:, g, samples],
-                        rhs=w2_codes[:, g, cols].bitcast(FP8X4),
-                        rhs_scale=w2_scales[:, g, cols],
-                        start=(g == 0),
-                        stop=(g == PASSES2 - 1),
-                    )
-
-        for m in range(SAMPLE_TILES):
-            samples = slice(m * P, (m + 1) * P)
-            for half in range(HID // BANK):
-                cols = slice(half * BANK, (half + 1) * BANK)
-                summed = out_pool.tile([P, BANK], F32)
-                nc.vector.tensor_tensor(out=summed[:], in0=out_ps[2 * m + half][:], in1=b2_all[:, cols], op=ALU.add)
-                result = out_pool.tile([P, BANK], F32)
-                nc.vector.scalar_tensor_tensor(
-                    out=result[:], in0=summed[:], scalar=SLOPE, in1=summed[:], op0=ALU.mult, op1=ALU.max
+            for b in range(OUT_BANKS):
+                m, half = divmod(b, HID // BANK)
+                nc.tensor.matmul_mx(
+                    out=out_ps[b][:],
+                    lhsT=h_codes[:, g, m * P : (m + 1) * P].bitcast(FP8X4),
+                    lhsT_scale=h_scales[:, g, m * P : (m + 1) * P],
+                    rhs=w2_codes[:, g, half * BANK : (half + 1) * BANK].bitcast(FP8X4),
+                    rhs_scale=w2_scales[:, g, half * BANK : (half + 1) * BANK],
+                    start=(g == 0),
+                    stop=(g == PASSES2 - 1),
                 )
-                nc.sync.dma_start(out=out[samples, cols], in_=result[:])
+
+        def leaky_and_store(b, summed):
+            result = out_pool.tile([P, BANK], F32, name="result")
+            nc.vector.scalar_tensor_tensor(
+                out=result[:], in0=summed[:], scalar=SLOPE, in1=summed[:], op0=ALU.mult, op1=ALU.max
+            )
+            m, half = divmod(b, HID // BANK)
+            nc.sync.dma_start(out=out[m * P : (m + 1) * P, half * BANK : (half + 1) * BANK], in_=result[:])
+
+        previous = None
+        for b in range(OUT_BANKS):
+            half = b % (HID // BANK)
+            summed = out_pool.tile([P, BANK], F32, name="summed")
+            nc.vector.tensor_tensor(
+                out=summed[:], in0=out_ps[b][:], in1=b2_all[:, half * BANK : (half + 1) * BANK], op=ALU.add
+            )
+            if previous is not None:
+                leaky_and_store(b - 1, previous)
+            previous = summed
+        leaky_and_store(OUT_BANKS - 1, previous)

@@ -29,11 +29,15 @@ HID_TILES = HID // P
 OUT_BANKS = BATCH * HID // (P * BANK)
 
 RUN = 4
-VECTOR_COLS = 496
-X_BANKS_PER_VECTOR_COPY = 4
+VECTOR_COLS = 480
+VECTOR_COLS_BESIDE_X = 608
 LAST_PIECES = 2
 RAW_BUFS = 6
 PIPE_BUFS = 3
+
+SPLIT_CHUNKS = 2
+CODE_BUFS = 4
+X_PASSES_PER_QUANTISE = 4
 
 FLOPS = 2 * BATCH * DIN * HID + 2 * BATCH * HID * HID
 
@@ -43,108 +47,106 @@ def tile_matchingnet_pb_k_kernel(tc, p, q, W1, b1, W2, b2, out):
     with ExitStack() as ctx:
         const = ctx.enter_context(tc.tile_pool(name="const", bufs=1))
         x_pool = ctx.enter_context(tc.tile_pool(name="x", bufs=1))
+        xg_pool = ctx.enter_context(tc.tile_pool(name="xg", bufs=1))
         raw_pool = ctx.enter_context(tc.tile_pool(name="raw", bufs=RAW_BUFS))
         grouped_pool = ctx.enter_context(tc.tile_pool(name="grouped", bufs=PIPE_BUFS))
-        w1_pool = ctx.enter_context(tc.tile_pool(name="w1", bufs=PIPE_BUFS))
+        w1_pool = ctx.enter_context(tc.tile_pool(name="w1", bufs=CODE_BUFS))
         w2_pool = ctx.enter_context(tc.tile_pool(name="w2", bufs=1))
         h_pool = ctx.enter_context(tc.tile_pool(name="h", bufs=1))
         out_pool = ctx.enter_context(tc.tile_pool(name="outs", bufs=OUT_BANKS))
         psum = ctx.enter_context(tc.psum_pool(name="psum", bufs=PSUM_BANKS))
         ctx.enter_context(tc.manual_schedule())
 
+        ident = const.tile([P, P], F32)
+        make_identity(nc, ident[:])
         b1_rows = const.tile([P, P], BF16)
-        nc.vector.memset(b1_rows[:], 0.0)
-        nc.sync.dma_start(out=b1_rows[0:HID_TILES, :], in_=b1.rearrange("(i a) -> i a", a=P))
+        nc.gpsimd.memset(b1_rows[:], 0.0)
         b2_row = const.tile([P, HID], BF16)
-        nc.vector.memset(b2_row[:], 0.0)
-        nc.sync.dma_start(out=b2_row[0:1, :], in_=b2.rearrange("(o n) -> o n", o=1))
+        nc.gpsimd.memset(b2_row[:], 0.0)
+        ones = const.tile([P, P], BF16)
+        nc.vector.memset(ones[:], 1.0)
+        b1_f32 = const.tile([P, P], F32)
+        b1_col = const.tile([P, HID_TILES], F32)
+        b2_all = const.tile([P, HID], BF16)
 
         p_tiles = p.rearrange("(m b) i j -> m b (i j)", b=P)
         q_tiles = q.rearrange("(m b) i j -> m b (i j)", b=P)
-        tables = []
-        for m in range(SAMPLE_TILES):
-            both = x_pool.tile([P, 2, TABLE], BF16, name="tables%d" % m)
-            for half in range(2):
-                cols = slice(half * TABLE // 2, (half + 1) * TABLE // 2)
-                nc.sync.dma_start(out=both[:, 0, cols], in_=p_tiles[m][:, cols])
-                nc.sync.dma_start(out=both[:, 1, cols], in_=q_tiles[m][:, cols])
-            tables.append(both)
-
-        ident = const.tile([P, P], F32)
-        make_identity(nc, ident[:])
-        ones = const.tile([P, P], BF16)
-        nc.vector.memset(ones[:], 1.0)
-
-        b1_f32 = const.tile([P, P], F32)
-        nc.vector.tensor_copy(out=b1_f32[:], in_=b1_rows[:])
-        b1_ps = psum.tile([P, P], F32, tag="bank")
-        nc.tensor.transpose(b1_ps[:], b1_f32[:], ident[:])
-        b1_col = const.tile([P, HID_TILES], F32)
-        nc.vector.tensor_copy(out=b1_col[:], in_=b1_ps[:, 0:HID_TILES])
-
-        b2_all = const.tile([P, HID], F32)
-        for half in range(HID // BANK):
-            cols = slice(half * BANK, (half + 1) * BANK)
-            b2_ps = psum.tile([P, BANK], F32, tag="bank")
-            nc.tensor.matmul(out=b2_ps[:], lhsT=ones[:], rhs=b2_row[:, cols], start=True, stop=True)
-            nc.scalar.activation(out=b2_all[:, cols], in_=b2_ps[:], func=ACT.Identity, scale=1.0)
-
         x_grouped = x_pool.tile([P, PASSES1, BATCH, PACK], BF16, align_bytes=64)
         x_grouped_words = x_grouped[:].bitcast(F32)
         x_codes = x_pool.tile([P, PASSES1, BATCH], U32, align_bytes=64)
         x_scales = x_pool.tile([P, PASSES1, BATCH], U8, align_bytes=64)
+        tables = [x_pool.tile([P, 2, TABLE], BF16, name="tables%d" % m) for m in range(SAMPLE_TILES)]
 
-        def quantise_x(pair, samples):
-            for g in (2 * pair, 2 * pair + 1):
-                nc.vector.quantize_mx(
-                    out=x_codes[:, g, samples].bitcast(FP8X4),
-                    scales=x_scales[:, g, samples],
-                    in_=x_grouped[:, g, samples, :].rearrange("a n t -> a (n t)"),
-                )
+        def load_x(half, m, pieces):
+            width = TABLE // 2 // pieces
+            for j in range(pieces):
+                cols = slice(half * TABLE // 2 + j * width, half * TABLE // 2 + (j + 1) * width)
+                nc.sync.dma_start(out=tables[m][:, 0, cols], in_=p_tiles[m][:, cols])
+                nc.sync.dma_start(out=tables[m][:, 1, cols], in_=q_tiles[m][:, cols])
 
-        for m in range(SAMPLE_TILES):
+        def regroup_x(half, m):
             samples = slice(m * P, (m + 1) * P)
             words = tables[m][:].bitcast(F32)
-            for pair in range(PASSES1 // 2):
+            for pair in range(half * PASSES1 // 4, (half + 1) * PASSES1 // 4):
                 xt = psum.tile([P, 2, 2, P], F32, tag="bank")
                 for gg in range(2):
                     g = 2 * pair + gg
                     for s in range(2):
                         nc.tensor.transpose(xt[:, gg, s, :], words[:, s, g * P : (g + 1) * P], ident[:])
-                if pair % X_BANKS_PER_VECTOR_COPY == X_BANKS_PER_VECTOR_COPY - 1:
-                    copy = nc.vector.tensor_copy
-                else:
-                    copy = nc.scalar.copy
-                copy(
+                nc.scalar.copy(
                     out=x_grouped_words[:, 2 * pair : 2 * pair + 2, samples, :],
                     in_=xt[:].rearrange("a g s n -> a g n s"),
                 )
-                if pair > 0:
-                    quantise_x(pair - 1, samples)
-            quantise_x(PASSES1 // 2 - 1, samples)
+
+        def quantise_x(half):
+            for g in range(half * PASSES1 // 2, (half + 1) * PASSES1 // 2, X_PASSES_PER_QUANTISE):
+                passes = slice(g, g + X_PASSES_PER_QUANTISE)
+                nc.vector.quantize_mx(
+                    out=x_codes[:, passes, :].rearrange("a g n -> a (g n)").bitcast(FP8X4),
+                    scales=x_scales[:, passes, :].rearrange("a g n -> a (g n)"),
+                    in_=x_grouped[:, passes, :, :].rearrange("a g n t -> a (g n t)"),
+                )
+
+        def load_biases():
+            nc.sync.dma_start(out=b1_rows[0:HID_TILES, :], in_=b1.rearrange("(i a) -> i a", a=P))
+            nc.sync.dma_start(out=b2_row[0:1, :], in_=b2.rearrange("(o n) -> o n", o=1))
+
+        spread = []
+
+        def spread_biases():
+            nc.gpsimd.tensor_copy(out=b1_f32[:], in_=b1_rows[:])
+            b1_ps = psum.tile([P, P], F32, tag="bank", name="b1_ps")
+            nc.tensor.transpose(b1_ps[:], b1_f32[:], ident[:])
+            b2_ps = psum.tile([P, HID], BF16, tag="bank", name="b2_ps")
+            for half in range(HID // BANK):
+                cols = slice(half * BANK, (half + 1) * BANK)
+                nc.tensor.matmul(out=b2_ps[:, cols], lhsT=ones[:], rhs=b2_row[:, cols], start=True, stop=True)
+            spread.extend([b1_ps, b2_ps])
+
+        def keep_biases():
+            nc.scalar.copy(out=b1_col[:], in_=spread[0][:, 0:HID_TILES])
+            nc.scalar.copy(out=b2_all[:], in_=spread[1][:])
 
         w1_chunks = W1.rearrange("(c a j) n -> c a j n", a=P, j=PACK)
         w2_chunks = W2.rearrange("(g t a) n -> g a t n", t=PACK, a=P)
         w2_codes = w2_pool.tile([P, PASSES2, HID], U32, align_bytes=64)
         w2_scales = w2_pool.tile([P, PASSES2, HID], U8, align_bytes=64)
-        acc = [psum.tile([P, BATCH], F32, tag="bank", name="acc%d" % i) for i in range(HID_TILES)]
         biased = [h_pool.tile([P, PACK, BATCH], F32, name="biased%d" % g) for g in range(PASSES2)]
 
-        last_width = HID // LAST_PIECES
-        pieces = [("W2", g, 0, HID) for g in range(PASSES2)]
-        pieces += [("W1", c, 0, HID) for c in range(PASSES1 - 1)]
-        pieces += [("W1", PASSES1 - 1, j * last_width, last_width) for j in range(LAST_PIECES)]
-
-        def load_and_regroup(matrix, chunk, first, width):
+        def load_w(matrix, chunk, first, width):
             raw = raw_pool.tile([P, PACK, width], BF16, tag="raw", name="raw")
+            chunks = w1_chunks if matrix == "W1" else w2_chunks
+            nc.sync.dma_start(out=raw[:], in_=chunks[chunk][:, :, first : first + width])
+            return raw
+
+        def regroup_w(matrix, raw, first, width, vector_cols):
             grouped = grouped_pool.tile([P, width, PACK], BF16, align_bytes=64, tag="grouped", name="grouped")
+            cols = raw[:, :, first : first + width]
             if matrix == "W1":
-                nc.sync.dma_start(out=raw[:], in_=w1_chunks[chunk][:, :, first : first + width])
-                rows = raw[:].rearrange("a (e s) n -> a s e n", s=2)
+                rows = cols.rearrange("a (e s) n -> a s e n", s=2)
             else:
-                nc.sync.dma_start(out=raw[:], in_=w2_chunks[chunk][:, :, first : first + width])
-                rows = raw[:].rearrange("a (s e) n -> a s e n", s=2)
-            split = width * VECTOR_COLS // HID
+                rows = cols.rearrange("a (s e) n -> a s e n", s=2)
+            split = width * vector_cols // HID
             nc.vector.tensor_copy(
                 out=grouped[:, 0:split, :].rearrange("a (c i) (s e) -> a c s e i", i=RUN, s=2),
                 in_=rows[:, :, :, 0:split].rearrange("a s e (c i) -> a c s e i", i=RUN),
@@ -155,23 +157,22 @@ def tile_matchingnet_pb_k_kernel(tc, p, q, W1, b1, W2, b2, out):
             )
             return grouped
 
-        def quantise_and_multiply(matrix, chunk, first, width, grouped):
+        def quantise_w(matrix, chunk, first, width, grouped):
             if matrix == "W2":
-                codes = w2_codes[:, chunk, :]
-                scales = w2_scales[:, chunk, :]
+                codes, scales = w2_codes[:, chunk, first : first + width], w2_scales[:, chunk, first : first + width]
             else:
                 codes = w1_pool.tile([P, width], U32, align_bytes=64, tag="codes", name="w1_codes")[:]
                 scales = w1_pool.tile([P, width], U8, align_bytes=64, tag="scales", name="w1_scales")[:]
             nc.vector.quantize_mx(
                 out=codes.bitcast(FP8X4), scales=scales, in_=grouped[:].rearrange("a n t -> a (n t)")
             )
-            if matrix == "W2":
-                return
+            return codes, scales
+
+        def multiply(chunk, first, width, codes, scales):
             for u in range(width // P):
-                i = first // P + u
                 units = slice(u * P, (u + 1) * P)
                 nc.tensor.matmul_mx(
-                    out=acc[i][:],
+                    out=acc[first // P + u][:],
                     lhsT=codes[:, units].bitcast(FP8X4),
                     lhsT_scale=scales[:, units],
                     rhs=x_codes[:, chunk, :].bitcast(FP8X4),
@@ -179,37 +180,102 @@ def tile_matchingnet_pb_k_kernel(tc, p, q, W1, b1, W2, b2, out):
                     start=(chunk == 0),
                     stop=(chunk == PASSES1 - 1),
                 )
-                if chunk == PASSES1 - 1:
-                    nc.scalar.activation(
-                        out=biased[i // PACK][:, i % PACK, :],
-                        in_=acc[i][:],
-                        func=ACT.Identity,
-                        bias=b1_col[:, i : i + 1],
-                        scale=1.0,
-                    )
 
-        waiting = None
-        for k in range(len(pieces)):
-            grouped = load_and_regroup(*pieces[k])
-            if k > 0:
-                quantise_and_multiply(*pieces[k - 1], waiting)
-            waiting = grouped
-        quantise_and_multiply(*pieces[-1], waiting)
+        def add_b1(i, on_vector):
+            target = biased[i // PACK][:, i % PACK, :]
+            if on_vector:
+                nc.vector.tensor_scalar_add(target, acc[i][:], b1_col[:, i : i + 1])
+            else:
+                nc.scalar.activation(out=target, in_=acc[i][:], func=ACT.Identity, bias=b1_col[:, i : i + 1], scale=1.0)
+
+        last = HID // LAST_PIECES
+        steps = [("W2", 0, 0), ("W2", 0, 1), ("X", 0, 0), ("W2", 1, None), ("X", 0, 1), ("W1", 0, None)]
+        steps += [("X", 1, 0), ("W1", 1, None), ("X", 1, 1)]
+        steps += [("W1", c, None) for c in range(2, PASSES1 - SPLIT_CHUNKS)]
+        steps += [("W1", c, j) for j in range(LAST_PIECES) for c in range(PASSES1 - SPLIT_CHUNKS, PASSES1)]
+        acc = []
+        ready = []
+        whole = {}
+
+        def columns(part):
+            return (0, HID) if part is None else (part * last, last)
+
+        def front(step):
+            kind, number, part = step
+            if kind == "X":
+                load_x(number, part, 1)
+                regroup_x(number, part)
+                return None
+            first, width = columns(part)
+            vector_cols = VECTOR_COLS if acc else VECTOR_COLS_BESIDE_X
+            if kind == "W1" and part is not None and number < PASSES1 - 1:
+                if part == 0:
+                    whole[number] = load_w(kind, number, 0, HID)
+                return regroup_w(kind, whole[number], first, width, vector_cols)
+            return regroup_w(kind, load_w(kind, number, first, width), 0, width, vector_cols)
+
+        def back(step, grouped):
+            kind, number, part = step
+            if kind == "X":
+                if part == 1:
+                    quantise_x(number)
+                if (number, part) == (1, 1):
+                    acc.extend([psum.tile([P, BATCH], F32, tag="bank", name="acc%d" % i) for i in range(HID_TILES)])
+            else:
+                first, width = columns(part)
+                codes, scales = quantise_w(kind, number, first, width, grouped)
+                if kind == "W1":
+                    ready.append((number, first, width, codes, scales))
+            if acc:
+                for item in ready:
+                    multiply(*item)
+                ready.clear()
+            if (kind, number, part) == ("W1", PASSES1 - 1, 0):
+                for i in range(PACK):
+                    add_b1(i, False)
 
         h_grouped = h_pool.tile([P, PASSES2, BATCH, PACK], BF16, align_bytes=64)
         h_codes = h_pool.tile([P, PASSES2, BATCH], U32, align_bytes=64)
         h_scales = h_pool.tile([P, PASSES2, BATCH], U8, align_bytes=64)
+
+        def leaky_h(g, samples):
+            by_sample = biased[g][:, :, samples].rearrange("a t n -> a n t")
+            nc.vector.scalar_tensor_tensor(
+                out=h_grouped[:, g, samples, :], in0=by_sample, scalar=SLOPE, in1=by_sample, op0=ALU.mult, op1=ALU.max
+            )
+
+        def quantise_h(g, samples):
+            nc.vector.quantize_mx(
+                out=h_codes[:, g, samples].bitcast(FP8X4),
+                scales=h_scales[:, g, samples],
+                in_=h_grouped[:, g, samples, :].rearrange("a n t -> a (n t)"),
+            )
+
+        waiting = front(steps[0])
+        for k in range(1, len(steps)):
+            grouped = front(steps[k])
+            back(steps[k - 1], waiting)
+            waiting = grouped
+            if k == 2:
+                load_biases()
+            elif k == 4:
+                spread_biases()
+            elif k == 5:
+                keep_biases()
+        everything = slice(0, BATCH)
+        leaky_h(0, everything)
+        back(steps[-1], waiting)
+        quantise_h(0, everything)
+        for i in range(PACK, HID_TILES):
+            add_b1(i, i % 2 == 1)
+
+        sample_tiles = [slice(m * P, (m + 1) * P) for m in range(SAMPLE_TILES)]
+        for samples in sample_tiles:
+            leaky_h(1, samples)
+        for samples in sample_tiles:
+            quantise_h(1, samples)
         out_ps = [psum.tile([P, BANK], F32, tag="bank", name="out_ps%d" % b) for b in range(OUT_BANKS)]
         for g in range(PASSES2):
-            by_sample = biased[g][:].rearrange("a t n -> a n t")
-            nc.vector.scalar_tensor_tensor(
-                out=h_grouped[:, g, :, :], in0=by_sample, scalar=SLOPE, in1=by_sample, op0=ALU.mult, op1=ALU.max
-            )
-            nc.vector.quantize_mx(
-                out=h_codes[:, g, :].bitcast(FP8X4),
-                scales=h_scales[:, g, :],
-                in_=h_grouped[:, g, :, :].rearrange("a n t -> a (n t)"),
-            )
             for b in range(OUT_BANKS):
                 m, half = divmod(b, HID // BANK)
                 nc.tensor.matmul_mx(

@@ -28,7 +28,7 @@ PASSES2 = HID // K_PASS
 HID_TILES = HID // P
 OUT_BANKS = BATCH * HID // (P * BANK)
 
-RUN = 4
+RUN = 8
 VECTOR_COLS = 480
 VECTOR_COLS_BESIDE_X = 608
 LAST_PIECES = 2

@@ -29,15 +29,20 @@ HID_TILES = HID // P
 OUT_BANKS = BATCH * HID // (P * BANK)
 
 RUN = 8
-VECTOR_COLS = 480
-VECTOR_COLS_BESIDE_X = 608
+VECTOR_COLS = 464
 LAST_PIECES = 2
-RAW_BUFS = 6
+RAW_BUFS = 7
 PIPE_BUFS = 3
 
-SPLIT_CHUNKS = 2
-CODE_BUFS = 4
-X_PASSES_PER_QUANTISE = 4
+SPLIT_CHUNKS = 3
+CODE_BUFS = 7
+QUARTERS = 4
+TABLE_BUFS = 2
+GROUPED_BUFS = 4
+FIRST_X_STEP = 4
+PASSES_X = PASSES1 // QUARTERS
+X_BANKS = 4
+VECTOR_X_BANKS = 1
 
 FLOPS = 2 * BATCH * DIN * HID + 2 * BATCH * HID * HID
 
@@ -47,9 +52,10 @@ def tile_matchingnet_pb_k_kernel(tc, p, q, W1, b1, W2, b2, out):
     with ExitStack() as ctx:
         const = ctx.enter_context(tc.tile_pool(name="const", bufs=1))
         x_pool = ctx.enter_context(tc.tile_pool(name="x", bufs=1))
-        xg_pool = ctx.enter_context(tc.tile_pool(name="xg", bufs=1))
+        table_pool = ctx.enter_context(tc.tile_pool(name="tables", bufs=TABLE_BUFS))
+        xg_pool = ctx.enter_context(tc.tile_pool(name="xg", bufs=PIPE_BUFS))
         raw_pool = ctx.enter_context(tc.tile_pool(name="raw", bufs=RAW_BUFS))
-        grouped_pool = ctx.enter_context(tc.tile_pool(name="grouped", bufs=PIPE_BUFS))
+        grouped_pool = ctx.enter_context(tc.tile_pool(name="grouped", bufs=GROUPED_BUFS))
         w1_pool = ctx.enter_context(tc.tile_pool(name="w1", bufs=CODE_BUFS))
         w2_pool = ctx.enter_context(tc.tile_pool(name="w2", bufs=1))
         h_pool = ctx.enter_context(tc.tile_pool(name="h", bufs=1))
@@ -69,43 +75,46 @@ def tile_matchingnet_pb_k_kernel(tc, p, q, W1, b1, W2, b2, out):
         b1_col = const.tile([P, HID_TILES], F32)
         b2_all = const.tile([P, HID], BF16)
 
-        p_tiles = p.rearrange("(m b) i j -> m b (i j)", b=P)
-        q_tiles = q.rearrange("(m b) i j -> m b (i j)", b=P)
-        x_grouped = x_pool.tile([P, PASSES1, BATCH, PACK], BF16, align_bytes=64)
-        x_grouped_words = x_grouped[:].bitcast(F32)
+        tables = [t.rearrange("(m b) i j -> b m (i j)", b=P) for t in (p, q)]
         x_codes = x_pool.tile([P, PASSES1, BATCH], U32, align_bytes=64)
         x_scales = x_pool.tile([P, PASSES1, BATCH], U8, align_bytes=64)
-        tables = [x_pool.tile([P, 2, TABLE], BF16, name="tables%d" % m) for m in range(SAMPLE_TILES)]
+        quarter_cols = TABLE // QUARTERS
+        quarters = []
 
-        def load_x(half, m, pieces):
-            width = TABLE // 2 // pieces
-            for j in range(pieces):
-                cols = slice(half * TABLE // 2 + j * width, half * TABLE // 2 + (j + 1) * width)
-                nc.sync.dma_start(out=tables[m][:, 0, cols], in_=p_tiles[m][:, cols])
-                nc.sync.dma_start(out=tables[m][:, 1, cols], in_=q_tiles[m][:, cols])
+        def load_x():
+            quarter = len(quarters)
+            both = table_pool.tile([P, 2, SAMPLE_TILES, quarter_cols], BF16, name="both")
+            cols = slice(quarter * quarter_cols, (quarter + 1) * quarter_cols)
+            for m in range(SAMPLE_TILES):
+                for s in range(2):
+                    nc.sync.dma_start(out=both[:, s, m, :], in_=tables[s][:, m, cols])
+            quarters.append(both)
 
-        def regroup_x(half, m):
-            samples = slice(m * P, (m + 1) * P)
-            words = tables[m][:].bitcast(F32)
-            for pair in range(half * PASSES1 // 4, (half + 1) * PASSES1 // 4):
-                xt = psum.tile([P, 2, 2, P], F32, tag="bank")
+        def regroup_x(quarter):
+            words = quarters[quarter][:].bitcast(F32)
+            grouped = xg_pool.tile([P, PASSES_X, BATCH, PACK], BF16, align_bytes=64, name="x_grouped")
+            grouped_words = grouped[:].bitcast(F32)
+            for b in range(X_BANKS):
+                m, pair = divmod(b, PASSES_X // 2)
+                xt = psum.tile([P, 2, 2, P], F32, tag="bank", name="xt")
                 for gg in range(2):
-                    g = 2 * pair + gg
+                    first = (2 * pair + gg) * P
                     for s in range(2):
-                        nc.tensor.transpose(xt[:, gg, s, :], words[:, s, g * P : (g + 1) * P], ident[:])
-                nc.scalar.copy(
-                    out=x_grouped_words[:, 2 * pair : 2 * pair + 2, samples, :],
+                        nc.tensor.transpose(xt[:, gg, s, :], words[:, s, m, first : first + P], ident[:])
+                copy = nc.vector.tensor_copy if b < VECTOR_X_BANKS else nc.scalar.copy
+                copy(
+                    out=grouped_words[:, 2 * pair : 2 * pair + 2, m * P : (m + 1) * P, :],
                     in_=xt[:].rearrange("a g s n -> a g n s"),
                 )
+            return grouped
 
-        def quantise_x(half):
-            for g in range(half * PASSES1 // 2, (half + 1) * PASSES1 // 2, X_PASSES_PER_QUANTISE):
-                passes = slice(g, g + X_PASSES_PER_QUANTISE)
-                nc.vector.quantize_mx(
-                    out=x_codes[:, passes, :].rearrange("a g n -> a (g n)").bitcast(FP8X4),
-                    scales=x_scales[:, passes, :].rearrange("a g n -> a (g n)"),
-                    in_=x_grouped[:, passes, :, :].rearrange("a g n t -> a (g n t)"),
-                )
+        def quantise_x(quarter, grouped):
+            passes = slice(PASSES_X * quarter, PASSES_X * (quarter + 1))
+            nc.vector.quantize_mx(
+                out=x_codes[:, passes, :].rearrange("a g n -> a (g n)").bitcast(FP8X4),
+                scales=x_scales[:, passes, :].rearrange("a g n -> a (g n)"),
+                in_=grouped[:].rearrange("a g n t -> a (g n t)"),
+            )
 
         def load_biases():
             nc.sync.dma_start(out=b1_rows[0:HID_TILES, :], in_=b1.rearrange("(i a) -> i a", a=P))
@@ -146,7 +155,7 @@ def tile_matchingnet_pb_k_kernel(tc, p, q, W1, b1, W2, b2, out):
                 rows = cols.rearrange("a (e s) n -> a s e n", s=2)
             else:
                 rows = cols.rearrange("a (s e) n -> a s e n", s=2)
-            split = width * vector_cols // HID
+            split = width * vector_cols // HID // RUN * RUN
             nc.vector.tensor_copy(
                 out=grouped[:, 0:split, :].rearrange("a (c i) (s e) -> a c s e i", i=RUN, s=2),
                 in_=rows[:, :, :, 0:split].rearrange("a s e (c i) -> a c s e i", i=RUN),
@@ -189,48 +198,47 @@ def tile_matchingnet_pb_k_kernel(tc, p, q, W1, b1, W2, b2, out):
                 nc.scalar.activation(out=target, in_=acc[i][:], func=ACT.Identity, bias=b1_col[:, i : i + 1], scale=1.0)
 
         last = HID // LAST_PIECES
-        steps = [("W2", 0, 0), ("W2", 0, 1), ("X", 0, 0), ("W2", 1, None), ("X", 0, 1), ("W1", 0, None)]
-        steps += [("X", 1, 0), ("W1", 1, None), ("X", 1, 1)]
-        steps += [("W1", c, None) for c in range(2, PASSES1 - SPLIT_CHUNKS)]
-        steps += [("W1", c, j) for j in range(LAST_PIECES) for c in range(PASSES1 - SPLIT_CHUNKS, PASSES1)]
+        pieces = [("W2", 0, 0, 256), ("W2", 0, 256, 256), ("W2", 1, 0, BANK)]
+        pieces += [("W1", c, 0, HID) for c in range(PASSES1 - SPLIT_CHUNKS)]
+        pieces += [("W1", c, j * last, last) for j in range(LAST_PIECES) for c in range(PASSES1 - SPLIT_CHUNKS, PASSES1)]
         acc = []
         ready = []
+        quantised = []
         whole = {}
 
-        def columns(part):
-            return (0, HID) if part is None else (part * last, last)
+        def load(step):
+            kind, number, first, width = pieces[step]
+            if kind == "W1" and PASSES1 - SPLIT_CHUNKS <= number < PASSES1 - 1:
+                if first == 0:
+                    whole[number] = load_w(kind, number, 0, HID)
+                return whole[number], first
+            return load_w(kind, number, first, width), 0
 
         def front(step):
-            kind, number, part = step
-            if kind == "X":
-                load_x(number, part, 1)
-                regroup_x(number, part)
-                return None
-            first, width = columns(part)
-            vector_cols = VECTOR_COLS if acc else VECTOR_COLS_BESIDE_X
-            if kind == "W1" and part is not None and number < PASSES1 - 1:
-                if part == 0:
-                    whole[number] = load_w(kind, number, 0, HID)
-                return regroup_w(kind, whole[number], first, width, vector_cols)
-            return regroup_w(kind, load_w(kind, number, first, width), 0, width, vector_cols)
+            kind, number, first, width = pieces[step]
+            quarter = step - FIRST_X_STEP
+            with_x = 0 <= quarter < QUARTERS
+            if with_x:
+                load_x()
+            raw, offset = load(step)
+            x_grouped = regroup_x(quarter) if with_x else None
+            return regroup_w(kind, raw, offset, width, VECTOR_COLS), x_grouped
 
-        def back(step, grouped):
-            kind, number, part = step
-            if kind == "X":
-                if part == 1:
-                    quantise_x(number)
-                if (number, part) == (1, 1):
+        def back(step, grouped, x_grouped):
+            kind, number, first, width = pieces[step]
+            codes, scales = quantise_w(kind, number, first, width, grouped)
+            if kind == "W1":
+                ready.append((number, first, width, codes, scales))
+            if x_grouped is not None:
+                quantise_x(len(quantised), x_grouped)
+                quantised.append(x_grouped)
+                if len(quantised) == QUARTERS:
                     acc.extend([psum.tile([P, BATCH], F32, tag="bank", name="acc%d" % i) for i in range(HID_TILES)])
-            else:
-                first, width = columns(part)
-                codes, scales = quantise_w(kind, number, first, width, grouped)
-                if kind == "W1":
-                    ready.append((number, first, width, codes, scales))
             if acc:
                 for item in ready:
                     multiply(*item)
                 ready.clear()
-            if (kind, number, part) == ("W1", PASSES1 - 1, 0):
+            if (kind, number, first) == ("W1", PASSES1 - SPLIT_CHUNKS, last):
                 for i in range(PACK):
                     add_b1(i, False)
 
@@ -251,23 +259,25 @@ def tile_matchingnet_pb_k_kernel(tc, p, q, W1, b1, W2, b2, out):
                 in_=h_grouped[:, g, samples, :].rearrange("a n t -> a (n t)"),
             )
 
-        waiting = front(steps[0])
-        for k in range(1, len(steps)):
-            grouped = front(steps[k])
-            back(steps[k - 1], waiting)
-            waiting = grouped
-            if k == 2:
+        waiting = front(0)
+        for k in range(1, len(pieces)):
+            fresh = front(k)
+            back(k - 1, *waiting)
+            waiting = fresh
+            if k == 4:
                 load_biases()
-            elif k == 4:
+            elif k == 6:
                 spread_biases()
-            elif k == 5:
+            elif k == 7:
                 keep_biases()
         everything = slice(0, BATCH)
         leaky_h(0, everything)
-        back(steps[-1], waiting)
+        back(len(pieces) - 1, *waiting)
         quantise_h(0, everything)
+        late = [regroup_w("W2", load_w("W2", 0, BANK, BANK), 0, BANK, VECTOR_COLS)]
         for i in range(PACK, HID_TILES):
             add_b1(i, i % 2 == 1)
+        late.append(regroup_w("W2", load_w("W2", 1, BANK, BANK), 0, BANK, VECTOR_COLS))
 
         sample_tiles = [slice(m * P, (m + 1) * P) for m in range(SAMPLE_TILES)]
         for samples in sample_tiles:
@@ -275,35 +285,46 @@ def tile_matchingnet_pb_k_kernel(tc, p, q, W1, b1, W2, b2, out):
         for samples in sample_tiles:
             quantise_h(1, samples)
         out_ps = [psum.tile([P, BANK], F32, tag="bank", name="out_ps%d" % b) for b in range(OUT_BANKS)]
-        for g in range(PASSES2):
-            for b in range(OUT_BANKS):
-                m, half = divmod(b, HID // BANK)
-                nc.tensor.matmul_mx(
-                    out=out_ps[b][:],
-                    lhsT=h_codes[:, g, m * P : (m + 1) * P].bitcast(FP8X4),
-                    lhsT_scale=h_scales[:, g, m * P : (m + 1) * P],
-                    rhs=w2_codes[:, g, half * BANK : (half + 1) * BANK].bitcast(FP8X4),
-                    rhs_scale=w2_scales[:, g, half * BANK : (half + 1) * BANK],
-                    start=(g == 0),
-                    stop=(g == PASSES2 - 1),
-                )
+
+        def stage2(g, b):
+            half, m = divmod(b, SAMPLE_TILES)
+            nc.tensor.matmul_mx(
+                out=out_ps[b][:],
+                lhsT=h_codes[:, g, m * P : (m + 1) * P].bitcast(FP8X4),
+                lhsT_scale=h_scales[:, g, m * P : (m + 1) * P],
+                rhs=w2_codes[:, g, half * BANK : (half + 1) * BANK].bitcast(FP8X4),
+                rhs_scale=w2_scales[:, g, half * BANK : (half + 1) * BANK],
+                start=(g == 0),
+                stop=(g == PASSES2 - 1),
+            )
+
+        def add_b2(b):
+            half = b // SAMPLE_TILES
+            summed = out_pool.tile([P, BANK], F32, name="summed")
+            nc.vector.tensor_tensor(
+                out=summed[:], in0=out_ps[b][:], in1=b2_all[:, half * BANK : (half + 1) * BANK], op=ALU.add
+            )
+            return summed
 
         def leaky_and_store(b, summed):
             result = out_pool.tile([P, BANK], F32, name="result")
             nc.vector.scalar_tensor_tensor(
                 out=result[:], in0=summed[:], scalar=SLOPE, in1=summed[:], op0=ALU.mult, op1=ALU.max
             )
-            m, half = divmod(b, HID // BANK)
+            half, m = divmod(b, SAMPLE_TILES)
             nc.sync.dma_start(out=out[m * P : (m + 1) * P, half * BANK : (half + 1) * BANK], in_=result[:])
 
-        previous = None
-        for b in range(OUT_BANKS):
-            half = b % (HID // BANK)
-            summed = out_pool.tile([P, BANK], F32, name="summed")
-            nc.vector.tensor_tensor(
-                out=summed[:], in0=out_ps[b][:], in1=b2_all[:, half * BANK : (half + 1) * BANK], op=ALU.add
-            )
-            if previous is not None:
-                leaky_and_store(b - 1, previous)
-            previous = summed
-        leaky_and_store(OUT_BANKS - 1, previous)
+        for g in range(PASSES2):
+            for b in range(SAMPLE_TILES):
+                stage2(g, b)
+        first_sums = [add_b2(b) for b in range(SAMPLE_TILES)]
+        for g in range(PASSES2):
+            quantise_w("W2", g, BANK, BANK, late[g])
+        for b in range(SAMPLE_TILES, OUT_BANKS):
+            for g in range(PASSES2):
+                stage2(g, b)
+        for b in range(SAMPLE_TILES):
+            leaky_and_store(b, first_sums[b])
+        last_sums = [add_b2(b) for b in range(SAMPLE_TILES, OUT_BANKS)]
+        for b in range(SAMPLE_TILES, OUT_BANKS):
+            leaky_and_store(b, last_sums[b - SAMPLE_TILES])

@@ -157,12 +157,12 @@ def tile_matchingnet_pb_k_kernel(tc, p, q, W1, b1, W2, b2, out):
                 rows = cols.rearrange("a (s e) n -> a s e n", s=2)
             split = width * vector_cols // HID // RUN * RUN
             nc.vector.tensor_copy(
-                out=grouped[:, 0:split, :].rearrange("a (c i) (s e) -> a c s e i", i=RUN, s=2),
-                in_=rows[:, :, :, 0:split].rearrange("a s e (c i) -> a c s e i", i=RUN),
+                out=grouped[:, 0:split, :].rearrange("a (c i) (s e) -> a c s i e", i=RUN, s=2),
+                in_=rows[:, :, :, 0:split].rearrange("a s e (c i) -> a c s i e", i=RUN),
             )
             nc.scalar.copy(
-                out=grouped[:, split:width, :].rearrange("a (c i) (s e) -> a c s e i", i=RUN, s=2),
-                in_=rows[:, :, :, split:width].rearrange("a s e (c i) -> a c s e i", i=RUN),
+                out=grouped[:, split:width, :].rearrange("a (c i) (s e) -> a c s i e", i=RUN, s=2),
+                in_=rows[:, :, :, split:width].rearrange("a s e (c i) -> a c s i e", i=RUN),
             )
             return grouped
 

from contextlib import ExitStack

import concourse.mybir as mybir
from concourse.masks import make_identity

F32 = mybir.dt.float32
BF16 = mybir.dt.bfloat16
U32 = mybir.dt.uint32
U8 = mybir.dt.uint8
FP8X4 = mybir.dt.float8_e4m3fn_x4
ALU = mybir.AluOpType
ACT = mybir.ActivationFunctionType

P = 128
PACK = 4
K_PASS = P * PACK
BANK = 512
PSUM_BANKS = 8

BATCH = 256
TABLE = 64 * 64
DIN = 2 * TABLE
HID = 1024
SLOPE = 0.01
SAMPLE_TILES = BATCH // P
PASSES1 = DIN // K_PASS
PASSES2 = HID // K_PASS
HID_TILES = HID // P
OUT_BANKS = BATCH * HID // (P * BANK)

RUN = 8
VECTOR_COLS = 464
LAST_PIECES = 2
RAW_BUFS = 7
PIPE_BUFS = 3

SPLIT_CHUNKS = 3
CODE_BUFS = 7
QUARTERS = 4
TABLE_BUFS = 2
GROUPED_BUFS = 4
FIRST_X_STEP = 4
PASSES_X = PASSES1 // QUARTERS
X_BANKS = 4
VECTOR_X_BANKS = 1

FLOPS = 2 * BATCH * DIN * HID + 2 * BATCH * HID * HID


def tile_matchingnet_pb_k_kernel(tc, p, q, W1, b1, W2, b2, out):
    nc = tc.nc
    with ExitStack() as ctx:
        const = ctx.enter_context(tc.tile_pool(name="const", bufs=1))
        x_pool = ctx.enter_context(tc.tile_pool(name="x", bufs=1))
        table_pool = ctx.enter_context(tc.tile_pool(name="tables", bufs=TABLE_BUFS))
        xg_pool = ctx.enter_context(tc.tile_pool(name="xg", bufs=PIPE_BUFS))
        raw_pool = ctx.enter_context(tc.tile_pool(name="raw", bufs=RAW_BUFS))
        grouped_pool = ctx.enter_context(tc.tile_pool(name="grouped", bufs=GROUPED_BUFS))
        w1_pool = ctx.enter_context(tc.tile_pool(name="w1", bufs=CODE_BUFS))
        w2_pool = ctx.enter_context(tc.tile_pool(name="w2", bufs=1))
        h_pool = ctx.enter_context(tc.tile_pool(name="h", bufs=1))
        out_pool = ctx.enter_context(tc.tile_pool(name="outs", bufs=OUT_BANKS))
        psum = ctx.enter_context(tc.psum_pool(name="psum", bufs=PSUM_BANKS))
        ctx.enter_context(tc.manual_schedule())

        ident = const.tile([P, P], F32)
        make_identity(nc, ident[:])
        b1_rows = const.tile([P, P], BF16)
        nc.gpsimd.memset(b1_rows[:], 0.0)
        b2_row = const.tile([P, HID], BF16)
        nc.gpsimd.memset(b2_row[:], 0.0)
        ones = const.tile([P, P], BF16)
        nc.vector.memset(ones[:], 1.0)
        b1_f32 = const.tile([P, P], F32)
        b1_col = const.tile([P, HID_TILES], F32)
        b2_all = const.tile([P, HID], BF16)

        tables = [t.rearrange("(m b) i j -> b m (i j)", b=P) for t in (p, q)]
        x_codes = x_pool.tile([P, PASSES1, BATCH], U32, align_bytes=64)
        x_scales = x_pool.tile([P, PASSES1, BATCH], U8, align_bytes=64)
        quarter_cols = TABLE // QUARTERS
        quarters = []

        def load_x():
            quarter = len(quarters)
            both = table_pool.tile([P, 2, SAMPLE_TILES, quarter_cols], BF16, name="both")
            cols = slice(quarter * quarter_cols, (quarter + 1) * quarter_cols)
            for m in range(SAMPLE_TILES):
                for s in range(2):
                    nc.sync.dma_start(out=both[:, s, m, :], in_=tables[s][:, m, cols])
            quarters.append(both)

        def regroup_x(quarter):
            words = quarters[quarter][:].bitcast(F32)
            grouped = xg_pool.tile([P, PASSES_X, BATCH, PACK], BF16, align_bytes=64, name="x_grouped")
            grouped_words = grouped[:].bitcast(F32)
            for b in range(X_BANKS):
                m, pair = divmod(b, PASSES_X // 2)
                xt = psum.tile([P, 2, 2, P], F32, tag="bank", name="xt")
                for gg in range(2):
                    first = (2 * pair + gg) * P
                    for s in range(2):
                        nc.tensor.transpose(xt[:, gg, s, :], words[:, s, m, first : first + P], ident[:])
                copy = nc.vector.tensor_copy if b < VECTOR_X_BANKS else nc.scalar.copy
                copy(
                    out=grouped_words[:, 2 * pair : 2 * pair + 2, m * P : (m + 1) * P, :],
                    in_=xt[:].rearrange("a g s n -> a g n s"),
                )
            return grouped

        def quantise_x(quarter, grouped):
            passes = slice(PASSES_X * quarter, PASSES_X * (quarter + 1))
            nc.vector.quantize_mx(
                out=x_codes[:, passes, :].rearrange("a g n -> a (g n)").bitcast(FP8X4),
                scales=x_scales[:, passes, :].rearrange("a g n -> a (g n)"),
                in_=grouped[:].rearrange("a g n t -> a (g n t)"),
            )

        def load_biases():
            nc.sync.dma_start(out=b1_rows[0:HID_TILES, :], in_=b1.rearrange("(i a) -> i a", a=P))
            nc.sync.dma_start(out=b2_row[0:1, :], in_=b2.rearrange("(o n) -> o n", o=1))

        spread = []

        def spread_biases():
            nc.gpsimd.tensor_copy(out=b1_f32[:], in_=b1_rows[:])
            b1_ps = psum.tile([P, P], F32, tag="bank", name="b1_ps")
            nc.tensor.transpose(b1_ps[:], b1_f32[:], ident[:])
            b2_ps = psum.tile([P, HID], BF16, tag="bank", name="b2_ps")
            for half in range(HID // BANK):
                cols = slice(half * BANK, (half + 1) * BANK)
                nc.tensor.matmul(out=b2_ps[:, cols], lhsT=ones[:], rhs=b2_row[:, cols], start=True, stop=True)
            spread.extend([b1_ps, b2_ps])

        def keep_biases():
            nc.scalar.copy(out=b1_col[:], in_=spread[0][:, 0:HID_TILES])
            nc.scalar.copy(out=b2_all[:], in_=spread[1][:])

        w1_chunks = W1.rearrange("(c a j) n -> c a j n", a=P, j=PACK)
        w2_chunks = W2.rearrange("(g t a) n -> g a t n", t=PACK, a=P)
        w2_codes = w2_pool.tile([P, PASSES2, HID], U32, align_bytes=64)
        w2_scales = w2_pool.tile([P, PASSES2, HID], U8, align_bytes=64)
        biased = [h_pool.tile([P, PACK, BATCH], F32, name="biased%d" % g) for g in range(PASSES2)]

        def load_w(matrix, chunk, first, width):
            raw = raw_pool.tile([P, PACK, width], BF16, tag="raw", name="raw")
            chunks = w1_chunks if matrix == "W1" else w2_chunks
            nc.sync.dma_start(out=raw[:], in_=chunks[chunk][:, :, first : first + width])
            return raw

        def regroup_w(matrix, raw, first, width, vector_cols):
            grouped = grouped_pool.tile([P, width, PACK], BF16, align_bytes=64, tag="grouped", name="grouped")
            cols = raw[:, :, first : first + width]
            if matrix == "W1":
                rows = cols.rearrange("a (e s) n -> a s e n", s=2)
            else:
                rows = cols.rearrange("a (s e) n -> a s e n", s=2)
            split = width * vector_cols // HID // RUN * RUN
            nc.vector.tensor_copy(
                out=grouped[:, 0:split, :].rearrange("a (c i) (s e) -> a c s i e", i=RUN, s=2),
                in_=rows[:, :, :, 0:split].rearrange("a s e (c i) -> a c s i e", i=RUN),
            )
            nc.scalar.copy(
                out=grouped[:, split:width, :].rearrange("a (c i) (s e) -> a c s i e", i=RUN, s=2),
                in_=rows[:, :, :, split:width].rearrange("a s e (c i) -> a c s i e", i=RUN),
            )
            return grouped

        def quantise_w(matrix, chunk, first, width, grouped):
            if matrix == "W2":
                codes, scales = w2_codes[:, chunk, first : first + width], w2_scales[:, chunk, first : first + width]
            else:
                codes = w1_pool.tile([P, width], U32, align_bytes=64, tag="codes", name="w1_codes")[:]
                scales = w1_pool.tile([P, width], U8, align_bytes=64, tag="scales", name="w1_scales")[:]
            nc.vector.quantize_mx(
                out=codes.bitcast(FP8X4), scales=scales, in_=grouped[:].rearrange("a n t -> a (n t)")
            )
            return codes, scales

        def multiply(chunk, first, width, codes, scales):
            for u in range(width // P):
                units = slice(u * P, (u + 1) * P)
                nc.tensor.matmul_mx(
                    out=acc[first // P + u][:],
                    lhsT=codes[:, units].bitcast(FP8X4),
                    lhsT_scale=scales[:, units],
                    rhs=x_codes[:, chunk, :].bitcast(FP8X4),
                    rhs_scale=x_scales[:, chunk, :],
                    start=(chunk == 0),
                    stop=(chunk == PASSES1 - 1),
                )

        def add_b1(i, on_vector):
            target = biased[i // PACK][:, i % PACK, :]
            if on_vector:
                nc.vector.tensor_scalar_add(target, acc[i][:], b1_col[:, i : i + 1])
            else:
                nc.scalar.activation(out=target, in_=acc[i][:], func=ACT.Identity, bias=b1_col[:, i : i + 1], scale=1.0)

        last = HID // LAST_PIECES
        pieces = [("W2", 0, 0, 256), ("W2", 0, 256, 256), ("W2", 1, 0, BANK)]
        pieces += [("W1", c, 0, HID) for c in range(PASSES1 - SPLIT_CHUNKS)]
        pieces += [("W1", c, j * last, last) for j in range(LAST_PIECES) for c in range(PASSES1 - SPLIT_CHUNKS, PASSES1)]
        acc = []
        ready = []
        quantised = []
        whole = {}

        def load(step):
            kind, number, first, width = pieces[step]
            if kind == "W1" and PASSES1 - SPLIT_CHUNKS <= number < PASSES1 - 1:
                if first == 0:
                    whole[number] = load_w(kind, number, 0, HID)
                return whole[number], first
            return load_w(kind, number, first, width), 0

        def front(step):
            kind, number, first, width = pieces[step]
            quarter = step - FIRST_X_STEP
            with_x = 0 <= quarter < QUARTERS
            if with_x:
                load_x()
            raw, offset = load(step)
            x_grouped = regroup_x(quarter) if with_x else None
            return regroup_w(kind, raw, offset, width, VECTOR_COLS), x_grouped

        def back(step, grouped, x_grouped):
            kind, number, first, width = pieces[step]
            codes, scales = quantise_w(kind, number, first, width, grouped)
            if kind == "W1":
                ready.append((number, first, width, codes, scales))
            if x_grouped is not None:
                quantise_x(len(quantised), x_grouped)
                quantised.append(x_grouped)
                if len(quantised) == QUARTERS:
                    acc.extend([psum.tile([P, BATCH], F32, tag="bank", name="acc%d" % i) for i in range(HID_TILES)])
            if acc:
                for item in ready:
                    multiply(*item)
                ready.clear()
            if (kind, number, first) == ("W1", PASSES1 - SPLIT_CHUNKS, last):
                for i in range(PACK):
                    add_b1(i, False)

        h_grouped = h_pool.tile([P, PASSES2, BATCH, PACK], BF16, align_bytes=64)
        h_codes = h_pool.tile([P, PASSES2, BATCH], U32, align_bytes=64)
        h_scales = h_pool.tile([P, PASSES2, BATCH], U8, align_bytes=64)

        def leaky_h(g, samples):
            by_sample = biased[g][:, :, samples].rearrange("a t n -> a n t")
            nc.vector.scalar_tensor_tensor(
                out=h_grouped[:, g, samples, :], in0=by_sample, scalar=SLOPE, in1=by_sample, op0=ALU.mult, op1=ALU.max
            )

        def quantise_h(g, samples):
            nc.vector.quantize_mx(
                out=h_codes[:, g, samples].bitcast(FP8X4),
                scales=h_scales[:, g, samples],
                in_=h_grouped[:, g, samples, :].rearrange("a n t -> a (n t)"),
            )

        waiting = front(0)
        for k in range(1, len(pieces)):
            fresh = front(k)
            back(k - 1, *waiting)
            waiting = fresh
            if k == 4:
                load_biases()
            elif k == 6:
                spread_biases()
            elif k == 7:
                keep_biases()
        everything = slice(0, BATCH)
        leaky_h(0, everything)
        back(len(pieces) - 1, *waiting)
        quantise_h(0, everything)
        late = [regroup_w("W2", load_w("W2", 0, BANK, BANK), 0, BANK, VECTOR_COLS)]
        for i in range(PACK, HID_TILES):
            add_b1(i, i % 2 == 1)
        late.append(regroup_w("W2", load_w("W2", 1, BANK, BANK), 0, BANK, VECTOR_COLS))

        sample_tiles = [slice(m * P, (m + 1) * P) for m in range(SAMPLE_TILES)]
        for samples in sample_tiles:
            leaky_h(1, samples)
        for samples in sample_tiles:
            quantise_h(1, samples)
        out_ps = [psum.tile([P, BANK], F32, tag="bank", name="out_ps%d" % b) for b in range(OUT_BANKS)]

        def stage2(g, b):
            half, m = divmod(b, SAMPLE_TILES)
            nc.tensor.matmul_mx(
                out=out_ps[b][:],
                lhsT=h_codes[:, g, m * P : (m + 1) * P].bitcast(FP8X4),
                lhsT_scale=h_scales[:, g, m * P : (m + 1) * P],
                rhs=w2_codes[:, g, half * BANK : (half + 1) * BANK].bitcast(FP8X4),
                rhs_scale=w2_scales[:, g, half * BANK : (half + 1) * BANK],
                start=(g == 0),
                stop=(g == PASSES2 - 1),
            )

        def add_b2(b):
            half = b // SAMPLE_TILES
            summed = out_pool.tile([P, BANK], F32, name="summed")
            nc.vector.tensor_tensor(
                out=summed[:], in0=out_ps[b][:], in1=b2_all[:, half * BANK : (half + 1) * BANK], op=ALU.add
            )
            return summed

        def leaky_and_store(b, summed):
            result = out_pool.tile([P, BANK], F32, name="result")
            nc.vector.scalar_tensor_tensor(
                out=result[:], in0=summed[:], scalar=SLOPE, in1=summed[:], op0=ALU.mult, op1=ALU.max
            )
            half, m = divmod(b, SAMPLE_TILES)
            nc.sync.dma_start(out=out[m * P : (m + 1) * P, half * BANK : (half + 1) * BANK], in_=result[:])

        for g in range(PASSES2):
            for b in range(SAMPLE_TILES):
                stage2(g, b)
        first_sums = [add_b2(b) for b in range(SAMPLE_TILES)]
        for g in range(PASSES2):
            quantise_w("W2", g, BANK, BANK, late[g])
        for b in range(SAMPLE_TILES, OUT_BANKS):
            for g in range(PASSES2):
                stage2(g, b)
        for b in range(SAMPLE_TILES):
            leaky_and_store(b, first_sums[b])
        last_sums = [add_b2(b) for b in range(SAMPLE_TILES, OUT_BANKS)]
        for b in range(SAMPLE_TILES, OUT_BANKS):
            leaky_and_store(b, last_sums[b - SAMPLE_TILES])
